import numpy as np
import ml_dtypes


def mxq(x, axis, fmt="e4m3"):
    dtype, down = {"e4m3": (ml_dtypes.float8_e4m3fn, 7), "e5m2": (ml_dtypes.float8_e5m2, 14)}[fmt]
    v = np.moveaxis(np.asarray(x, np.float32).astype(ml_dtypes.bfloat16).astype(np.float64), axis, -1)
    blocks = v.reshape(v.shape[:-1] + (-1, 32))
    amax = np.abs(blocks).max(-1, keepdims=True)
    byte = np.maximum(np.where(amax > 0, np.frexp(amax)[1] - 1 + 127, 0) - down, 1)
    scale = np.exp2(byte - 127.0)
    codes = (blocks / scale).astype(np.float32).astype(dtype).astype(np.float64)
    return np.moveaxis((codes * scale).reshape(v.shape), -1, axis)


WIDE = False


def mx_kscale(k):
    if not WIDE:
        return np.ones(k)
    levels = np.array([10, -10, 5, -5, 0])
    a = np.random.permutation(np.resize(levels, k // 512 * 4)).reshape(k // 512, 4)
    idx = np.arange(k)
    return np.exp2(a[idx // 512, idx % 128 // 32])


BF16 = ml_dtypes.bfloat16


def bf(x):
    return np.asarray(x, np.float32).astype(BF16)


def f64(x):
    return np.asarray(x).astype(np.float64)


B, G, Z1, Z2, H, PD = 4096, 4, 256, 256, 512, 128


def glin(x, W, b):
    y = mxq(x, 2, "e4m3").transpose(1, 0, 2) @ mxq(f64(W), 2, "e4m3").transpose(0, 2, 1)
    return y.transpose(1, 0, 2) + f64(b)


def setup_inputs():
    s = mx_kscale(H)
    h = np.maximum(np.random.standard_normal((B, G, H)), 0.0) + np.maximum(np.random.standard_normal((B, G, H)), 0.0)
    return {"h": bf(h * s),
            "W3": bf(np.random.standard_normal((G, H, H)) / np.sqrt(H) * s[None, :, None] / s[None, None, :]),
            "b3": bf(np.random.standard_normal((G, H)) * 0.2 * s),
            "Wo": bf(np.random.standard_normal((G, PD, H)) * 0.6 / np.sqrt(H) / s[None, None, :]),
            "bo": bf(np.random.standard_normal((G, PD)) * 0.2)}


def reference(h, W3, b3, Wo, bo):
    h = f64(h)
    h3 = np.maximum(glin(h, W3, b3), 0.0) + h
    out = glin(h3, Wo, bo)
    return out.reshape(B, G * PD)

@@ -1,0 +1,148 @@
+from contextlib import ExitStack
+
+import concourse.mybir as mybir
+from concourse.masks import make_identity
+
+F32 = mybir.dt.float32
+BF16 = mybir.dt.bfloat16
+I32 = mybir.dt.int32
+U32 = mybir.dt.uint32
+U8 = mybir.dt.uint8
+FP8X4 = mybir.dt.float8_e4m3fn_x4
+ADD = mybir.AluOpType.add
+RELU = mybir.ActivationFunctionType.Relu
+
+B, G, H, PD = 4096, 4, 512, 128
+P = 128
+PACK = 4
+ROW_TILES = 4
+UNIT = P * ROW_TILES
+CHUNKS = B // UNIT
+WORDS = H // 2
+
+FLOPS = 2 * B * G * (H * H + H * PD)
+
+
+def quantise_rows(nc, pools, identity, rows, codes, scales):
+    row_words = rows[:].bitcast(F32)
+    grouped = pools["grouped"].tile([P, UNIT * PACK], BF16, align_bytes=64)
+    grouped_words = grouped[:].bitcast(F32).rearrange("p (c u) -> p c u", u=2)
+    for pair in range(ROW_TILES // 2):
+        turned = pools["turned"].tile([P, 2, 2 * P], F32)
+        for j in range(2):
+            for u in range(2):
+                first = ((2 * pair + j) * 2 + u) * P
+                nc.tensor.transpose(
+                    turned[:, u, j * P : (j + 1) * P], row_words[:, first : first + P], identity[:]
+                )
+        nc.scalar.copy(
+            out=grouped_words[:, pair * 2 * P : (pair + 1) * 2 * P, :],
+            in_=turned[:].rearrange("p u c -> p c u"),
+        )
+    nc.vector.quantize_mx(out=codes.bitcast(FP8X4), scales=scales, in_=grouped[:])
+    return grouped
+
+
+def tile_linearwdecoder_pb_t_kernel(tc, h, W3, b3, Wo, bo, out):
+    nc = tc.nc
+    with ExitStack() as ctx:
+        const = ctx.enter_context(tc.tile_pool(name="const", bufs=1))
+        pools = {
+            "rows": ctx.enter_context(tc.tile_pool(name="rows", bufs=8)),
+            "grouped": ctx.enter_context(tc.tile_pool(name="grouped", bufs=4)),
+            "weights": ctx.enter_context(tc.tile_pool(name="weights", bufs=2)),
+            "mx": ctx.enter_context(tc.tile_pool(name="mx", bufs=3)),
+            "relu": ctx.enter_context(tc.tile_pool(name="relu", bufs=3)),
+            "result": ctx.enter_context(tc.tile_pool(name="result", bufs=4)),
+            "turned": ctx.enter_context(tc.psum_pool(name="turned", bufs=2)),
+            "hidden": ctx.enter_context(tc.psum_pool(name="hidden", bufs=4)),
+            "projected": ctx.enter_context(tc.psum_pool(name="projected", bufs=2)),
+        }
+
+        identity = const.tile([P, P], F32)
+        make_identity(nc, identity[:])
+
+        h_units = h.rearrange("(c p i) g k -> c g p i k", p=P, i=ROW_TILES)
+        out_units = out.rearrange("(c p i) (g n) -> c g p i n", p=P, i=ROW_TILES, g=G)
+        w3_units = W3.rearrange("g (a p e) k -> g p a (e k)", a=2, e=2)
+        wo_unit = Wo.rearrange("g p k -> p g k")
+
+        def load_rows(view):
+            rows = pools["rows"].tile([P, UNIT * PACK], BF16)
+            nc.sync.dma_start(out=rows[:].rearrange("p (i k) -> p i k", i=view.shape[1]), in_=view)
+            return rows
+
+        b3_rows = const.tile([P, 2 * P], BF16)
+        nc.vector.memset(b3_rows[:].bitcast(I32), 0)
+        nc.scalar.dma_start(out=b3_rows[0 : 2 * G, :], in_=b3.rearrange("g (a w) -> (g a) w", a=2))
+        bo_rows = const.tile([P, G * PD], BF16)
+        nc.scalar.dma_start(out=bo_rows[:], in_=bo.rearrange("g n -> (g n)").partition_broadcast(P))
+
+        wo_codes = const.tile([P, UNIT], U32, align_bytes=64)
+        wo_scales = const.tile([P, UNIT], U8, align_bytes=64)
+
+        b3_turned = pools["turned"].tile([P, 2, 2 * P], F32, tag="turned")
+        nc.tensor.transpose(b3_turned[:, 0, 0:P], b3_rows[:].bitcast(F32), identity[:])
+        b3_words = const.tile([P, 2 * G], F32)
+        nc.scalar.copy(out=b3_words[:], in_=b3_turned[:, 0, 0 : 2 * G])
+        b3_columns = const.tile([P, PACK * G], F32)
+        nc.vector.tensor_copy(out=b3_columns[:], in_=b3_words[:].bitcast(BF16))
+
+        quantise_rows(nc, pools, identity, load_rows(wo_unit), wo_codes[:], wo_scales[:])
+
+        for g in range(G):
+            w3_codes = pools["weights"].tile([P, UNIT], U32, align_bytes=64)
+            w3_scales = pools["weights"].tile([P, UNIT], U8, align_bytes=64)
+            quantise_rows(nc, pools, identity, load_rows(w3_units[g]), w3_codes[:], w3_scales[:])
+
+            for c in range(CHUNKS):
+                h_codes = pools["mx"].tile([P, UNIT], U32, align_bytes=64)
+                h_scales = pools["mx"].tile([P, UNIT], U8, align_bytes=64)
+                h_turned = quantise_rows(nc, pools, identity, load_rows(h_units[c, g]), h_codes[:], h_scales[:])
+
+                relu = pools["relu"].tile([P, PACK, UNIT], F32)
+                for t in range(PACK):
+                    hidden = pools["hidden"].tile([P, UNIT], F32)
+                    nc.tensor.matmul_mx(
+                        out=hidden[:],
+                        lhsT=w3_codes[:, t * P : (t + 1) * P].bitcast(FP8X4),
+                        lhsT_scale=w3_scales[:, t * P : (t + 1) * P],
+                        rhs=h_codes[:].bitcast(FP8X4),
+                        rhs_scale=h_scales[:],
+                        start=True,
+                        stop=True,
+                    )
+                    nc.scalar.activation(
+                        out=relu[:, t, :], in_=hidden[:], func=RELU, bias=b3_columns[:, PACK * g + t : PACK * g + t + 1]
+                    )
+
+                h3 = pools["grouped"].tile([P, UNIT * PACK], BF16, align_bytes=64)
+                nc.vector.tensor_tensor(
+                    out=h3[:].rearrange("p (c t) -> p c t", t=PACK),
+                    in0=relu[:].rearrange("p t c -> p c t"),
+                    in1=h_turned[:].rearrange("p (c t) -> p c t", t=PACK),
+                    op=ADD,
+                )
+                h3_codes = pools["mx"].tile([P, UNIT], U32, align_bytes=64)
+                h3_scales = pools["mx"].tile([P, UNIT], U8, align_bytes=64)
+                nc.vector.quantize_mx(out=h3_codes[:].bitcast(FP8X4), scales=h3_scales[:], in_=h3[:])
+
+                projected = pools["projected"].tile([P, ROW_TILES, PD], F32)
+                for i in range(ROW_TILES):
+                    nc.tensor.matmul_mx(
+                        out=projected[:, i, :],
+                        lhsT=h3_codes[:, i * P : (i + 1) * P].bitcast(FP8X4),
+                        lhsT_scale=h3_scales[:, i * P : (i + 1) * P],
+                        rhs=wo_codes[:, g * PD : (g + 1) * PD].bitcast(FP8X4),
+                        rhs_scale=wo_scales[:, g * PD : (g + 1) * PD],
+                        start=True,
+                        stop=True,
+                    )
+                result = pools["result"].tile([P, ROW_TILES, PD], F32)
+                nc.vector.tensor_tensor(
+                    out=result[:],
+                    in0=projected[:],
+                    in1=bo_rows[:, g * PD : (g + 1) * PD].unsqueeze(1).to_broadcast([P, ROW_TILES, PD]),
+                    op=ADD,
+                )
+                nc.sync.dma_start(out=out_units[c, g], in_=result[:])

@@ -18,131 +18,194 @@ PACK = 4
 ROW_TILES = 4
 UNIT = P * ROW_TILES
 CHUNKS = B // UNIT
-WORDS = H // 2
 
 FLOPS = 2 * B * G * (H * H + H * PD)
-
-
-def quantise_rows(nc, pools, identity, rows, codes, scales):
-    row_words = rows[:].bitcast(F32)
-    grouped = pools["grouped"].tile([P, UNIT * PACK], BF16, align_bytes=64)
-    grouped_words = grouped[:].bitcast(F32).rearrange("p (c u) -> p c u", u=2)
-    for pair in range(ROW_TILES // 2):
-        turned = pools["turned"].tile([P, 2, 2 * P], F32)
-        for j in range(2):
-            for u in range(2):
-                first = ((2 * pair + j) * 2 + u) * P
-                nc.tensor.transpose(
-                    turned[:, u, j * P : (j + 1) * P], row_words[:, first : first + P], identity[:]
-                )
-        nc.scalar.copy(
-            out=grouped_words[:, pair * 2 * P : (pair + 1) * 2 * P, :],
-            in_=turned[:].rearrange("p u c -> p c u"),
-        )
-    nc.vector.quantize_mx(out=codes.bitcast(FP8X4), scales=scales, in_=grouped[:])
-    return grouped
 
 
 def tile_linearwdecoder_pb_t_kernel(tc, h, W3, b3, Wo, bo, out):
     nc = tc.nc
     with ExitStack() as ctx:
         const = ctx.enter_context(tc.tile_pool(name="const", bufs=1))
-        pools = {
-            "rows": ctx.enter_context(tc.tile_pool(name="rows", bufs=8)),
-            "grouped": ctx.enter_context(tc.tile_pool(name="grouped", bufs=4)),
-            "weights": ctx.enter_context(tc.tile_pool(name="weights", bufs=2)),
-            "mx": ctx.enter_context(tc.tile_pool(name="mx", bufs=3)),
-            "relu": ctx.enter_context(tc.tile_pool(name="relu", bufs=3)),
-            "result": ctx.enter_context(tc.tile_pool(name="result", bufs=4)),
-            "turned": ctx.enter_context(tc.psum_pool(name="turned", bufs=2)),
-            "hidden": ctx.enter_context(tc.psum_pool(name="hidden", bufs=4)),
-            "projected": ctx.enter_context(tc.psum_pool(name="projected", bufs=2)),
-        }
+        weights = ctx.enter_context(tc.tile_pool(name="weights", bufs=G + 1))
+        rows_pool = ctx.enter_context(tc.tile_pool(name="rows", bufs=6))
+        grouped_pool = ctx.enter_context(tc.tile_pool(name="grouped", bufs=5))
+        mx_pool = ctx.enter_context(tc.tile_pool(name="mx", bufs=3))
+        relu_pool = ctx.enter_context(tc.tile_pool(name="relu", bufs=3))
+        h3_pool = ctx.enter_context(tc.tile_pool(name="h3", bufs=2))
+        result_pool = ctx.enter_context(tc.tile_pool(name="result", bufs=3))
+        turned_pool = ctx.enter_context(tc.psum_pool(name="turned", bufs=2))
+        hidden_pool = ctx.enter_context(tc.psum_pool(name="hidden", bufs=PACK))
+        projected_pool = ctx.enter_context(tc.psum_pool(name="projected", bufs=2))
 
         identity = const.tile([P, P], F32)
         make_identity(nc, identity[:])
 
-        h_units = h.rearrange("(c p i) g k -> c g p i k", p=P, i=ROW_TILES)
-        out_units = out.rearrange("(c p i) (g n) -> c g p i n", p=P, i=ROW_TILES, g=G)
-        w3_units = W3.rearrange("g (a p e) k -> g p a (e k)", a=2, e=2)
-        wo_unit = Wo.rearrange("g p k -> p g k")
-
-        def load_rows(view):
-            rows = pools["rows"].tile([P, UNIT * PACK], BF16)
-            nc.sync.dma_start(out=rows[:].rearrange("p (i k) -> p i k", i=view.shape[1]), in_=view)
-            return rows
-
         b3_rows = const.tile([P, 2 * P], BF16)
         nc.vector.memset(b3_rows[:].bitcast(I32), 0)
         nc.scalar.dma_start(out=b3_rows[0 : 2 * G, :], in_=b3.rearrange("g (a w) -> (g a) w", a=2))
-        bo_rows = const.tile([P, G * PD], BF16)
-        nc.scalar.dma_start(out=bo_rows[:], in_=bo.rearrange("g n -> (g n)").partition_broadcast(P))
-
-        wo_codes = const.tile([P, UNIT], U32, align_bytes=64)
-        wo_scales = const.tile([P, UNIT], U8, align_bytes=64)
-
-        b3_turned = pools["turned"].tile([P, 2, 2 * P], F32, tag="turned")
+        b3_turned = turned_pool.tile([P, 2, 2 * P], F32, tag="turned")
         nc.tensor.transpose(b3_turned[:, 0, 0:P], b3_rows[:].bitcast(F32), identity[:])
         b3_words = const.tile([P, 2 * G], F32)
         nc.scalar.copy(out=b3_words[:], in_=b3_turned[:, 0, 0 : 2 * G])
         b3_columns = const.tile([P, PACK * G], F32)
         nc.vector.tensor_copy(out=b3_columns[:], in_=b3_words[:].bitcast(BF16))
+        bo_rows = const.tile([P, G * PD], BF16)
+        nc.scalar.dma_start(out=bo_rows[:], in_=bo.rearrange("g n -> (g n)").partition_broadcast(P))
 
-        quantise_rows(nc, pools, identity, load_rows(wo_unit), wo_codes[:], wo_scales[:])
+        h_units = h.rearrange("(c p i) g k -> c g p i k", p=P, i=ROW_TILES)
+        out_units = out.rearrange("(c p i) (g n) -> c g p i n", p=P, i=ROW_TILES, g=G)
+        w3_units = W3.rearrange("g (a p e) k -> g p a (e k)", a=2, e=2)
 
+        stream = [(Wo.rearrange("g p k -> p g k"), None, None)]
+        w3_place = []
         for g in range(G):
-            w3_codes = pools["weights"].tile([P, UNIT], U32, align_bytes=64)
-            w3_scales = pools["weights"].tile([P, UNIT], U8, align_bytes=64)
-            quantise_rows(nc, pools, identity, load_rows(w3_units[g]), w3_codes[:], w3_scales[:])
-
+            w3_place.append(len(stream))
+            stream.append((w3_units[g], g, None))
             for c in range(CHUNKS):
-                h_codes = pools["mx"].tile([P, UNIT], U32, align_bytes=64)
-                h_scales = pools["mx"].tile([P, UNIT], U8, align_bytes=64)
-                h_turned = quantise_rows(nc, pools, identity, load_rows(h_units[c, g]), h_codes[:], h_scales[:])
+                stream.append((h_units[c, g], g, c))
+        tiles = {}
 
-                relu = pools["relu"].tile([P, PACK, UNIT], F32)
-                for t in range(PACK):
-                    hidden = pools["hidden"].tile([P, UNIT], F32)
-                    nc.tensor.matmul_mx(
-                        out=hidden[:],
-                        lhsT=w3_codes[:, t * P : (t + 1) * P].bitcast(FP8X4),
-                        lhsT_scale=w3_scales[:, t * P : (t + 1) * P],
-                        rhs=h_codes[:].bitcast(FP8X4),
-                        rhs_scale=h_scales[:],
-                        start=True,
-                        stop=True,
-                    )
-                    nc.scalar.activation(
-                        out=relu[:, t, :], in_=hidden[:], func=RELU, bias=b3_columns[:, PACK * g + t : PACK * g + t + 1]
-                    )
+        def in_stream(n):
+            return 0 <= n < len(stream)
 
-                h3 = pools["grouped"].tile([P, UNIT * PACK], BF16, align_bytes=64)
-                nc.vector.tensor_tensor(
-                    out=h3[:].rearrange("p (c t) -> p c t", t=PACK),
-                    in0=relu[:].rearrange("p t c -> p c t"),
-                    in1=h_turned[:].rearrange("p (c t) -> p c t", t=PACK),
-                    op=ADD,
+        def is_tokens(n):
+            return in_stream(n) and stream[n][2] is not None
+
+        def load(n):
+            if not in_stream(n):
+                return
+            view = stream[n][0]
+            rows = rows_pool.tile([P, UNIT * PACK], BF16)
+            nc.sync.dma_start(out=rows[:].rearrange("p (i k) -> p i k", i=view.shape[1]), in_=view)
+            tiles["rows", n] = rows
+
+        def turn(n):
+            if not in_stream(n):
+                return
+            row_words = tiles["rows", n][:].bitcast(F32)
+            for pair in range(ROW_TILES // 2):
+                turned = turned_pool.tile([P, 2, 2 * P], F32)
+                for j in range(2):
+                    for u in range(2):
+                        first = ((2 * pair + j) * 2 + u) * P
+                        nc.tensor.transpose(
+                            turned[:, u, j * P : (j + 1) * P], row_words[:, first : first + P], identity[:]
+                        )
+                tiles["turned", n, pair] = turned
+
+        def regroup(n):
+            if not in_stream(n):
+                return
+            grouped = grouped_pool.tile([P, UNIT * PACK], BF16, align_bytes=64)
+            grouped_words = grouped[:].bitcast(F32).rearrange("p (c u) -> p c u", u=2)
+            for pair in range(ROW_TILES // 2):
+                nc.scalar.copy(
+                    out=grouped_words[:, pair * 2 * P : (pair + 1) * 2 * P, :],
+                    in_=tiles["turned", n, pair][:].rearrange("p u c -> p c u"),
                 )
-                h3_codes = pools["mx"].tile([P, UNIT], U32, align_bytes=64)
-                h3_scales = pools["mx"].tile([P, UNIT], U8, align_bytes=64)
-                nc.vector.quantize_mx(out=h3_codes[:].bitcast(FP8X4), scales=h3_scales[:], in_=h3[:])
+            tiles["grouped", n] = grouped
 
-                projected = pools["projected"].tile([P, ROW_TILES, PD], F32)
-                for i in range(ROW_TILES):
-                    nc.tensor.matmul_mx(
-                        out=projected[:, i, :],
-                        lhsT=h3_codes[:, i * P : (i + 1) * P].bitcast(FP8X4),
-                        lhsT_scale=h3_scales[:, i * P : (i + 1) * P],
-                        rhs=wo_codes[:, g * PD : (g + 1) * PD].bitcast(FP8X4),
-                        rhs_scale=wo_scales[:, g * PD : (g + 1) * PD],
-                        start=True,
-                        stop=True,
-                    )
-                result = pools["result"].tile([P, ROW_TILES, PD], F32)
-                nc.vector.tensor_tensor(
-                    out=result[:],
-                    in0=projected[:],
-                    in1=bo_rows[:, g * PD : (g + 1) * PD].unsqueeze(1).to_broadcast([P, ROW_TILES, PD]),
-                    op=ADD,
+        def quantise(n):
+            if not in_stream(n):
+                return
+            pool = mx_pool if is_tokens(n) else weights
+            codes = pool.tile([P, UNIT], U32, align_bytes=64)
+            scales = pool.tile([P, UNIT], U8, align_bytes=64)
+            nc.vector.quantize_mx(out=codes[:].bitcast(FP8X4), scales=scales[:], in_=tiles["grouped", n][:])
+            tiles["codes", n] = codes
+            tiles["scales", n] = scales
+
+        def multiply_w3(n):
+            if not is_tokens(n):
+                return
+            w3 = w3_place[stream[n][1]]
+            for t in range(PACK):
+                hidden = hidden_pool.tile([P, UNIT], F32)
+                nc.tensor.matmul_mx(
+                    out=hidden[:],
+                    lhsT=tiles["codes", w3][:, t * P : (t + 1) * P].bitcast(FP8X4),
+                    lhsT_scale=tiles["scales", w3][:, t * P : (t + 1) * P],
+                    rhs=tiles["codes", n][:].bitcast(FP8X4),
+                    rhs_scale=tiles["scales", n][:],
+                    start=True,
+                    stop=True,
                 )
-                nc.sync.dma_start(out=out_units[c, g], in_=result[:])
+                tiles["hidden", n, t] = hidden
+
+        def bias_relu(n):
+            if not is_tokens(n):
+                return
+            g = stream[n][1]
+            relu = relu_pool.tile([P, PACK, UNIT], F32)
+            for t in range(PACK):
+                nc.scalar.activation(
+                    out=relu[:, t, :],
+                    in_=tiles["hidden", n, t][:],
+                    func=RELU,
+                    bias=b3_columns[:, PACK * g + t : PACK * g + t + 1],
+                )
+            tiles["relu", n] = relu
+
+        def add_residual(n):
+            if not is_tokens(n):
+                return
+            h3 = h3_pool.tile([P, UNIT * PACK], BF16, align_bytes=64)
+            nc.vector.tensor_tensor(
+                out=h3[:].rearrange("p (c t) -> p c t", t=PACK),
+                in0=tiles["relu", n][:].rearrange("p t c -> p c t"),
+                in1=tiles["grouped", n][:].rearrange("p (c t) -> p c t", t=PACK),
+                op=ADD,
+            )
+            tiles["h3", n] = h3
+
+        def quantise_h3(n):
+            if not is_tokens(n):
+                return
+            h3_codes = h3_pool.tile([P, UNIT], U32, align_bytes=64)
+            h3_scales = h3_pool.tile([P, UNIT], U8, align_bytes=64)
+            nc.vector.quantize_mx(out=h3_codes[:].bitcast(FP8X4), scales=h3_scales[:], in_=tiles["h3", n][:])
+            tiles["h3_codes", n] = h3_codes
+            tiles["h3_scales", n] = h3_scales
+
+        def multiply_wo(n):
+            if not is_tokens(n):
+                return
+            g = stream[n][1]
+            projected = projected_pool.tile([P, ROW_TILES, PD], F32)
+            for i in range(ROW_TILES):
+                nc.tensor.matmul_mx(
+                    out=projected[:, i, :],
+                    lhsT=tiles["h3_codes", n][:, i * P : (i + 1) * P].bitcast(FP8X4),
+                    lhsT_scale=tiles["h3_scales", n][:, i * P : (i + 1) * P],
+                    rhs=tiles["codes", 0][:, g * PD : (g + 1) * PD].bitcast(FP8X4),
+                    rhs_scale=tiles["scales", 0][:, g * PD : (g + 1) * PD],
+                    start=True,
+                    stop=True,
+                )
+            tiles["projected", n] = projected
+
+        def finish(n):
+            if not is_tokens(n):
+                return
+            g, c = stream[n][1], stream[n][2]
+            result = result_pool.tile([P, ROW_TILES, PD], F32)
+            nc.vector.tensor_tensor(
+                out=result[:],
+                in0=tiles["projected", n][:],
+                in1=bo_rows[:, g * PD : (g + 1) * PD].unsqueeze(1).to_broadcast([P, ROW_TILES, PD]),
+                op=ADD,
+            )
+            nc.sync.dma_start(out=out_units[c, g], in_=result[:])
+
+        with tc.manual_schedule():
+            for step in range(len(stream) + 7):
+                load(step)
+                quantise(step - 4)
+                turn(step - 3)
+                multiply_wo(step - 7)
+                bias_relu(step - 5)
+                multiply_w3(step - 4)
+                regroup(step - 3)
+                add_residual(step - 6)
+                finish(step - 7)
+                quantise_h3(step - 6)

@@ -18,6 +18,7 @@ PACK = 4
 ROW_TILES = 4
 UNIT = P * ROW_TILES
 CHUNKS = B // UNIT
+RUN = 4
 
 FLOPS = 2 * B * G * (H * H + H * PD)
 
@@ -151,9 +152,9 @@ def tile_linearwdecoder_pb_t_kernel(tc, h, W3, b3, Wo, bo, out):
                 return
             h3 = h3_pool.tile([P, UNIT * PACK], BF16, align_bytes=64)
             nc.vector.tensor_tensor(
-                out=h3[:].rearrange("p (c t) -> p c t", t=PACK),
-                in0=tiles["relu", n][:].rearrange("p t c -> p c t"),
-                in1=tiles["grouped", n][:].rearrange("p (c t) -> p c t", t=PACK),
+                out=h3[:].rearrange("p (c i t) -> p c t i", i=RUN, t=PACK),
+                in0=tiles["relu", n][:].rearrange("p t (c i) -> p c t i", i=RUN),
+                in1=tiles["grouped", n][:].rearrange("p (c i t) -> p c t i", i=RUN, t=PACK),
                 op=ADD,
             )
             tiles["h3", n] = h3

@@ -5,7 +5,6 @@ from concourse.masks import make_identity
 
 F32 = mybir.dt.float32
 BF16 = mybir.dt.bfloat16
-I32 = mybir.dt.int32
 U32 = mybir.dt.uint32
 U8 = mybir.dt.uint8
 FP8X4 = mybir.dt.float8_e4m3fn_x4
@@ -41,18 +40,6 @@ def tile_linearwdecoder_pb_t_kernel(tc, h, W3, b3, Wo, bo, out):
         identity = const.tile([P, P], F32)
         make_identity(nc, identity[:])
 
-        b3_rows = const.tile([P, 2 * P], BF16)
-        nc.vector.memset(b3_rows[:].bitcast(I32), 0)
-        nc.scalar.dma_start(out=b3_rows[0 : 2 * G, :], in_=b3.rearrange("g (a w) -> (g a) w", a=2))
-        b3_turned = turned_pool.tile([P, 2, 2 * P], F32, tag="turned")
-        nc.tensor.transpose(b3_turned[:, 0, 0:P], b3_rows[:].bitcast(F32), identity[:])
-        b3_words = const.tile([P, 2 * G], F32)
-        nc.scalar.copy(out=b3_words[:], in_=b3_turned[:, 0, 0 : 2 * G])
-        b3_columns = const.tile([P, PACK * G], F32)
-        nc.vector.tensor_copy(out=b3_columns[:], in_=b3_words[:].bitcast(BF16))
-        bo_rows = const.tile([P, G * PD], BF16)
-        nc.scalar.dma_start(out=bo_rows[:], in_=bo.rearrange("g n -> (g n)").partition_broadcast(P))
-
         h_units = h.rearrange("(c p i) g k -> c g p i k", p=P, i=ROW_TILES)
         out_units = out.rearrange("(c p i) (g n) -> c g p i n", p=P, i=ROW_TILES, g=G)
         w3_units = W3.rearrange("g (a p e) k -> g p a (e k)", a=2, e=2)
@@ -72,6 +59,9 @@ def tile_linearwdecoder_pb_t_kernel(tc, h, W3, b3, Wo, bo, out):
         def is_tokens(n):
             return in_stream(n) and stream[n][2] is not None
 
+        def is_w3(n):
+            return in_stream(n) and stream[n][1] is not None and stream[n][2] is None
+
         def load(n):
             if not in_stream(n):
                 return
@@ -79,6 +69,17 @@ def tile_linearwdecoder_pb_t_kernel(tc, h, W3, b3, Wo, bo, out):
             rows = rows_pool.tile([P, UNIT * PACK], BF16)
             nc.sync.dma_start(out=rows[:].rearrange("p (i k) -> p i k", i=view.shape[1]), in_=view)
             tiles["rows", n] = rows
+            if is_w3(n):
+                g = stream[n][1]
+                b3_pairs = weights.tile([P, PACK], BF16)
+                nc.scalar.dma_start(
+                    out=b3_pairs[:].rearrange("p (a e) -> p a e", a=2),
+                    in_=b3[g].rearrange("(a p e) -> p a e", a=2, e=2),
+                )
+                bo_rows = weights.tile([P, PD], BF16)
+                nc.scalar.dma_start(out=bo_rows[:], in_=bo[g].partition_broadcast(P))
+                tiles["b3_pairs", g] = b3_pairs
+                tiles["bo_rows", g] = bo_rows
 
         def turn(n):
             if not in_stream(n):
@@ -115,6 +116,11 @@ def tile_linearwdecoder_pb_t_kernel(tc, h, W3, b3, Wo, bo, out):
             nc.vector.quantize_mx(out=codes[:].bitcast(FP8X4), scales=scales[:], in_=tiles["grouped", n][:])
             tiles["codes", n] = codes
             tiles["scales", n] = scales
+            if is_w3(n):
+                g = stream[n][1]
+                b3_columns = weights.tile([P, PACK], F32)
+                nc.vector.tensor_copy(out=b3_columns[:], in_=tiles["b3_pairs", g][:])
+                tiles["b3_columns", g] = b3_columns
 
         def multiply_w3(n):
             if not is_tokens(n):
@@ -143,7 +149,7 @@ def tile_linearwdecoder_pb_t_kernel(tc, h, W3, b3, Wo, bo, out):
                     out=relu[:, t, :],
                     in_=tiles["hidden", n, t][:],
                     func=RELU,
-                    bias=b3_columns[:, PACK * g + t : PACK * g + t + 1],
+                    bias=tiles["b3_columns", g][:, t : t + 1],
                 )
             tiles["relu", n] = relu
 
@@ -193,7 +199,7 @@ def tile_linearwdecoder_pb_t_kernel(tc, h, W3, b3, Wo, bo, out):
             nc.vector.tensor_tensor(
                 out=result[:],
                 in0=tiles["projected", n][:],
-                in1=bo_rows[:, g * PD : (g + 1) * PD].unsqueeze(1).to_broadcast([P, ROW_TILES, PD]),
+                in1=tiles["bo_rows", g][:].unsqueeze(1).to_broadcast([P, ROW_TILES, PD]),
                 op=ADD,
             )
             nc.sync.dma_start(out=out_units[c, g], in_=result[:])

from contextlib import ExitStack

import concourse.mybir as mybir
from concourse.masks import make_identity

F32 = mybir.dt.float32
BF16 = mybir.dt.bfloat16
U32 = mybir.dt.uint32
U8 = mybir.dt.uint8
FP8X4 = mybir.dt.float8_e4m3fn_x4
ADD = mybir.AluOpType.add
RELU = mybir.ActivationFunctionType.Relu

B, G, H, PD = 4096, 4, 512, 128
P = 128
PACK = 4
ROW_TILES = 4
UNIT = P * ROW_TILES
CHUNKS = B // UNIT
RUN = 4

FLOPS = 2 * B * G * (H * H + H * PD)


def tile_linearwdecoder_pb_t_kernel(tc, h, W3, b3, Wo, bo, out):
    nc = tc.nc
    with ExitStack() as ctx:
        const = ctx.enter_context(tc.tile_pool(name="const", bufs=1))
        weights = ctx.enter_context(tc.tile_pool(name="weights", bufs=G + 1))
        rows_pool = ctx.enter_context(tc.tile_pool(name="rows", bufs=6))
        grouped_pool = ctx.enter_context(tc.tile_pool(name="grouped", bufs=5))
        mx_pool = ctx.enter_context(tc.tile_pool(name="mx", bufs=3))
        relu_pool = ctx.enter_context(tc.tile_pool(name="relu", bufs=3))
        h3_pool = ctx.enter_context(tc.tile_pool(name="h3", bufs=2))
        result_pool = ctx.enter_context(tc.tile_pool(name="result", bufs=3))
        turned_pool = ctx.enter_context(tc.psum_pool(name="turned", bufs=2))
        hidden_pool = ctx.enter_context(tc.psum_pool(name="hidden", bufs=PACK))
        projected_pool = ctx.enter_context(tc.psum_pool(name="projected", bufs=2))

        identity = const.tile([P, P], F32)
        make_identity(nc, identity[:])

        h_units = h.rearrange("(c p i) g k -> c g p i k", p=P, i=ROW_TILES)
        out_units = out.rearrange("(c p i) (g n) -> c g p i n", p=P, i=ROW_TILES, g=G)
        w3_units = W3.rearrange("g (a p e) k -> g p a (e k)", a=2, e=2)

        stream = [(Wo.rearrange("g p k -> p g k"), None, None)]
        w3_place = []
        for g in range(G):
            w3_place.append(len(stream))
            stream.append((w3_units[g], g, None))
            for c in range(CHUNKS):
                stream.append((h_units[c, g], g, c))
        tiles = {}

        def in_stream(n):
            return 0 <= n < len(stream)

        def is_tokens(n):
            return in_stream(n) and stream[n][2] is not None

        def is_w3(n):
            return in_stream(n) and stream[n][1] is not None and stream[n][2] is None

        def load(n):
            if not in_stream(n):
                return
            view = stream[n][0]
            rows = rows_pool.tile([P, UNIT * PACK], BF16)
            nc.sync.dma_start(out=rows[:].rearrange("p (i k) -> p i k", i=view.shape[1]), in_=view)
            tiles["rows", n] = rows
            if is_w3(n):
                g = stream[n][1]
                b3_pairs = weights.tile([P, PACK], BF16)
                nc.scalar.dma_start(
                    out=b3_pairs[:].rearrange("p (a e) -> p a e", a=2),
                    in_=b3[g].rearrange("(a p e) -> p a e", a=2, e=2),
                )
                bo_rows = weights.tile([P, PD], BF16)
                nc.scalar.dma_start(out=bo_rows[:], in_=bo[g].partition_broadcast(P))
                tiles["b3_pairs", g] = b3_pairs
                tiles["bo_rows", g] = bo_rows

        def turn(n):
            if not in_stream(n):
                return
            row_words = tiles["rows", n][:].bitcast(F32)
            for pair in range(ROW_TILES // 2):
                turned = turned_pool.tile([P, 2, 2 * P], F32)
                for j in range(2):
                    for u in range(2):
                        first = ((2 * pair + j) * 2 + u) * P
                        nc.tensor.transpose(
                            turned[:, u, j * P : (j + 1) * P], row_words[:, first : first + P], identity[:]
                        )
                tiles["turned", n, pair] = turned

        def regroup(n):
            if not in_stream(n):
                return
            grouped = grouped_pool.tile([P, UNIT * PACK], BF16, align_bytes=64)
            grouped_words = grouped[:].bitcast(F32).rearrange("p (c u) -> p c u", u=2)
            for pair in range(ROW_TILES // 2):
                nc.scalar.copy(
                    out=grouped_words[:, pair * 2 * P : (pair + 1) * 2 * P, :],
                    in_=tiles["turned", n, pair][:].rearrange("p u c -> p c u"),
                )
            tiles["grouped", n] = grouped

        def quantise(n):
            if not in_stream(n):
                return
            pool = mx_pool if is_tokens(n) else weights
            codes = pool.tile([P, UNIT], U32, align_bytes=64)
            scales = pool.tile([P, UNIT], U8, align_bytes=64)
            nc.vector.quantize_mx(out=codes[:].bitcast(FP8X4), scales=scales[:], in_=tiles["grouped", n][:])
            tiles["codes", n] = codes
            tiles["scales", n] = scales
            if is_w3(n):
                g = stream[n][1]
                b3_columns = weights.tile([P, PACK], F32)
                nc.vector.tensor_copy(out=b3_columns[:], in_=tiles["b3_pairs", g][:])
                tiles["b3_columns", g] = b3_columns

        def multiply_w3(n):
            if not is_tokens(n):
                return
            w3 = w3_place[stream[n][1]]
            for t in range(PACK):
                hidden = hidden_pool.tile([P, UNIT], F32)
                nc.tensor.matmul_mx(
                    out=hidden[:],
                    lhsT=tiles["codes", w3][:, t * P : (t + 1) * P].bitcast(FP8X4),
                    lhsT_scale=tiles["scales", w3][:, t * P : (t + 1) * P],
                    rhs=tiles["codes", n][:].bitcast(FP8X4),
                    rhs_scale=tiles["scales", n][:],
                    start=True,
                    stop=True,
                )
                tiles["hidden", n, t] = hidden

        def bias_relu(n):
            if not is_tokens(n):
                return
            g = stream[n][1]
            relu = relu_pool.tile([P, PACK, UNIT], F32)
            for t in range(PACK):
                nc.scalar.activation(
                    out=relu[:, t, :],
                    in_=tiles["hidden", n, t][:],
                    func=RELU,
                    bias=tiles["b3_columns", g][:, t : t + 1],
                )
            tiles["relu", n] = relu

        def add_residual(n):
            if not is_tokens(n):
                return
            h3 = h3_pool.tile([P, UNIT * PACK], BF16, align_bytes=64)
            nc.vector.tensor_tensor(
                out=h3[:].rearrange("p (c i t) -> p c t i", i=RUN, t=PACK),
                in0=tiles["relu", n][:].rearrange("p t (c i) -> p c t i", i=RUN),
                in1=tiles["grouped", n][:].rearrange("p (c i t) -> p c t i", i=RUN, t=PACK),
                op=ADD,
            )
            tiles["h3", n] = h3

        def quantise_h3(n):
            if not is_tokens(n):
                return
            h3_codes = h3_pool.tile([P, UNIT], U32, align_bytes=64)
            h3_scales = h3_pool.tile([P, UNIT], U8, align_bytes=64)
            nc.vector.quantize_mx(out=h3_codes[:].bitcast(FP8X4), scales=h3_scales[:], in_=tiles["h3", n][:])
            tiles["h3_codes", n] = h3_codes
            tiles["h3_scales", n] = h3_scales

        def multiply_wo(n):
            if not is_tokens(n):
                return
            g = stream[n][1]
            projected = projected_pool.tile([P, ROW_TILES, PD], F32)
            for i in range(ROW_TILES):
                nc.tensor.matmul_mx(
                    out=projected[:, i, :],
                    lhsT=tiles["h3_codes", n][:, i * P : (i + 1) * P].bitcast(FP8X4),
                    lhsT_scale=tiles["h3_scales", n][:, i * P : (i + 1) * P],
                    rhs=tiles["codes", 0][:, g * PD : (g + 1) * PD].bitcast(FP8X4),
                    rhs_scale=tiles["scales", 0][:, g * PD : (g + 1) * PD],
                    start=True,
                    stop=True,
                )
            tiles["projected", n] = projected

        def finish(n):
            if not is_tokens(n):
                return
            g, c = stream[n][1], stream[n][2]
            result = result_pool.tile([P, ROW_TILES, PD], F32)
            nc.vector.tensor_tensor(
                out=result[:],
                in0=tiles["projected", n][:],
                in1=tiles["bo_rows", g][:].unsqueeze(1).to_broadcast([P, ROW_TILES, PD]),
                op=ADD,
            )
            nc.sync.dma_start(out=out_units[c, g], in_=result[:])

        with tc.manual_schedule():
            for step in range(len(stream) + 7):
                load(step)
                quantise(step - 4)
                turn(step - 3)
                multiply_wo(step - 7)
                bias_relu(step - 5)
                multiply_w3(step - 4)
                regroup(step - 3)
                add_residual(step - 6)
                finish(step - 7)
                quantise_h3(step - 6)
